import numpy as np
import ml_dtypes


def mxq(x, axis, fmt="e4m3"):
    dtype, down = {"e4m3": (ml_dtypes.float8_e4m3fn, 7), "e5m2": (ml_dtypes.float8_e5m2, 14)}[fmt]
    v = np.moveaxis(np.asarray(x, np.float32).astype(ml_dtypes.bfloat16).astype(np.float64), axis, -1)
    blocks = v.reshape(v.shape[:-1] + (-1, 32))
    amax = np.abs(blocks).max(-1, keepdims=True)
    byte = np.maximum(np.where(amax > 0, np.frexp(amax)[1] - 1 + 127, 0) - down, 1)
    scale = np.exp2(byte - 127.0)
    codes = (blocks / scale).astype(np.float32).astype(dtype).astype(np.float64)
    return np.moveaxis((codes * scale).reshape(v.shape), -1, axis)


WIDE = False


def mx_kscale(k):
    if not WIDE:
        return np.ones(k)
    levels = np.array([10, -10, 5, -5, 0])
    a = np.random.permutation(np.resize(levels, k // 512 * 4)).reshape(k // 512, 4)
    idx = np.arange(k)
    return np.exp2(a[idx // 512, idx % 128 // 32])


BF16 = ml_dtypes.bfloat16


def bf(x):
    return np.asarray(x, np.float32).astype(BF16)


def f64(x):
    return np.asarray(x).astype(np.float64)


B, N, M, D = 4, 1024, 1024, 512


def sigmoid(x):
    return 1.0 / (1.0 + np.exp(-x))


def setup_inputs():
    s = mx_kscale(M)
    wq = np.random.standard_normal((D, D + 1)) / np.sqrt(D)
    wq[:, D] *= np.sqrt(D)
    return {"encoded_last_node": bf(np.random.standard_normal((B, N, D))),
            "load": bf(np.random.random((B, N))),
            "cur_dist": bf(np.random.random((B, N, M))),
            "log_scale": bf(2.0 + 0.1 * np.random.standard_normal(1)),
            "ninf_mask": bf(np.where(np.random.random((B, N, M)) < 0.25, -6.0, 0.0) + np.log(s)),
            "k": bf(np.random.standard_normal((B, M, D)) - np.log(s)[:, None]),
            "v": bf(np.random.standard_normal((B, M, D)) * 3.0),
            "Wq_last": bf(wq),
            "alpha1": bf(1.5 + 0.1 * np.random.standard_normal(1))}


def reference(encoded_last_node, load, cur_dist, log_scale, ninf_mask, k, v, Wq_last, alpha1):
    wq = f64(Wq_last)
    q = f64(encoded_last_node) @ wq[:, :D].T + f64(load)[:, :, None] * wq[:, D]
    eb = np.exp(-f64(alpha1)[0] * f64(log_scale)[0] * f64(cur_dist) + f64(ninf_mask))
    ek = np.exp(f64(k))
    ebq = mxq(eb, 2, "e4m3")
    num = ebq @ mxq(ek * f64(v), 1, "e4m3")
    den = ebq @ mxq(ek, 1, "e4m3")
    return sigmoid(q) * (num / den)

@@ -1,0 +1,346 @@
+from contextlib import ExitStack
+
+import concourse.mybir as mybir
+from concourse.masks import make_identity
+
+F32 = mybir.dt.float32
+BF16 = mybir.dt.bfloat16
+U32 = mybir.dt.uint32
+U8 = mybir.dt.uint8
+FP8X4 = mybir.dt.float8_e4m3fn_x4
+ACT = mybir.ActivationFunctionType
+ALU = mybir.AluOpType
+
+B, N, M, D = 4, 1024, 1024, 512
+FLOPS = 2 * B * N * D * (D + 1) + 2 * 2 * B * N * M * D
+
+P = 128
+PACK = 4
+K_PASS = P * PACK
+PASSES = M // K_PASS
+TILES_PER_BATCH = N // P
+TILES = B * TILES_PER_BATCH
+LOAD_TILES = 4
+F_CHUNKS = D // P
+BLOCKS_PER_MATMUL = M // P // F_CHUNKS
+PIECE = P
+PIECES_PER_PASS = D // PIECE
+PIECES_PER_BATCH = PASSES * PIECES_PER_PASS
+PIECES = B * PIECES_PER_BATCH
+assert PIECES_PER_BATCH == TILES_PER_BATCH
+
+EXPONENT_LEAD = 3
+TRANSPOSE_LEAD = 2
+EXP_LEAD = 1
+NUM_LAG = 1
+MERGE_LAG = 2
+LN_LAG = 1
+RECIP_LAG = TILES_PER_BATCH + LN_LAG
+FINISH_LAG = RECIP_LAG + 1
+LOAD_LEAD = EXPONENT_LEAD + 3
+KEY_LEAD = PIECES_PER_BATCH
+KEY_LOAD_LEAD = KEY_LEAD + 3
+FIRST_STEP = -KEY_LOAD_LEAD
+LAST_STEP = TILES - 1 + FINISH_LAG
+
+
+def tile_cvrp_decoder_pa_t_kernel(
+    tc, encoded_last_node, load, cur_dist, log_scale, ninf_mask, k, v, Wq_last, alpha1, out
+):
+    nc = tc.nc
+
+    dist_view = cur_dist.rearrange("b (p i) m -> b p i m", i=TILES_PER_BATCH)
+    mask_view = ninf_mask.rearrange("b (p i) m -> b p i m", i=TILES_PER_BATCH)
+    node_view = encoded_last_node.rearrange("b (p i) f -> b p i f", i=TILES_PER_BATCH)
+    out_view = out.rearrange("b (p i) d -> b p i d", i=TILES_PER_BATCH)
+    k_view = k.rearrange("b (g t p) d -> b g p t d", g=PASSES, t=PACK)
+    v_view = v.rearrange("b (g t p) d -> b g p t d", g=PASSES, t=PACK)
+
+    with ExitStack() as ctx:
+        ctx.enter_context(tc.manual_schedule())
+        consts = ctx.enter_context(tc.tile_pool(name="consts", bufs=1))
+        loads = ctx.enter_context(tc.tile_pool(name="loads", bufs=2))
+        codes = ctx.enter_context(tc.tile_pool(name="codes", bufs=2))
+        stage = ctx.enter_context(tc.tile_pool(name="stage", bufs=3))
+        gates = ctx.enter_context(tc.tile_pool(name="gates", bufs=FINISH_LAG + 2))
+        logs = ctx.enter_context(tc.tile_pool(name="logs", bufs=TILES_PER_BATCH + 2))
+        psum_xt = ctx.enter_context(tc.psum_pool(name="psum_xt", bufs=3))
+        psum_et = ctx.enter_context(tc.psum_pool(name="psum_et", bufs=1))
+        psum_q = ctx.enter_context(tc.psum_pool(name="psum_q", bufs=2))
+        psum_acc = ctx.enter_context(tc.psum_pool(name="psum_acc", bufs=2))
+
+        ident_f32 = consts.tile([P, P], F32, name="ident_f32")
+        make_identity(nc, ident_f32[:])
+        ident_bf16 = consts.tile([P, P], BF16, name="ident_bf16")
+        make_identity(nc, ident_bf16[:])
+
+        alpha_all = consts.tile([P, 1], BF16, name="alpha_all")
+        nc.sync.dma_start(out=alpha_all[:], in_=alpha1.partition_broadcast(P))
+        scale_all = consts.tile([P, 1], BF16, name="scale_all")
+        nc.sync.dma_start(out=scale_all[:], in_=log_scale.partition_broadcast(P))
+        neg_slope = consts.tile([P, 1], F32, name="neg_slope")
+        nc.vector.scalar_tensor_tensor(
+            out=neg_slope[:], in0=alpha_all[:], scalar=-1.0, in1=scale_all[:],
+            op0=ALU.mult, op1=ALU.mult,
+        )
+
+        load_rows = consts.tile([P, B * N], BF16, name="load_rows")
+        nc.vector.memset(load_rows[:], 0.0)
+        nc.sync.dma_start(
+            out=load_rows[P - 1 : P, :], in_=load.rearrange("(o b) n -> o (b n)", o=1)
+        )
+        load_by_tile = load_rows[:].rearrange(
+            "q (b p i) -> q b i p", b=B, i=TILES_PER_BATCH
+        )
+
+        wq_rows = consts.tile([P, F_CHUNKS, D + 2], BF16, name="wq_rows")
+        nc.sync.dma_start(
+            out=wq_rows[:, :, 0 : D + 1], in_=Wq_last.rearrange("(t p) f -> p t f", p=P)
+        )
+        wq_t = consts.tile([P, F_CHUNKS + 1, D], BF16, name="wq_t")
+        for c in range(F_CHUNKS + 1):
+            first = min(c * P, D + 1 - P)
+            et = psum_et.tile([P, F_CHUNKS, P], BF16, name="et")
+            for t in range(F_CHUNKS):
+                nc.tensor.transpose(et[:, t, :], wq_rows[:, t, first : first + P], ident_bf16[:])
+            nc.vector.tensor_copy(
+                out=wq_t[:, c, :], in_=et[:].rearrange("p t d -> p (t d)")
+            )
+
+        halves = {}
+        key_loads = {}
+        key_exp = {}
+        key_codes = {}
+        score_codes = {}
+        exponents = {}
+        transposed = {}
+        scores = {}
+        node_ps = {}
+        node_t = {}
+        q_ps = {}
+        num_ps = {}
+        gate = {}
+        log_den = {}
+
+        def is_tile(t):
+            return 0 <= t < TILES
+
+        def is_piece(piece):
+            return 0 <= piece < PIECES
+
+        def load_queries(h):
+            b, first = divmod(h * LOAD_TILES, TILES_PER_BATCH)
+            rows = slice(first, first + LOAD_TILES)
+            dist = loads.tile([P, LOAD_TILES, M], BF16, name="dist")
+            nc.sync.dma_start(out=dist[:], in_=dist_view[b, :, rows, :])
+            mask = loads.tile([P, LOAD_TILES, M], BF16, name="mask")
+            nc.sync.dma_start(out=mask[:], in_=mask_view[b, :, rows, :])
+            node = loads.tile([P, LOAD_TILES, D], BF16, name="node")
+            nc.sync.dma_start(out=node[:], in_=node_view[b, :, rows, :])
+            halves[h] = (dist, mask, node)
+
+        def load_keys(b, g):
+            k_rows = loads.tile([P, PACK, D], BF16, name="k_rows")
+            nc.sync.dma_start(out=k_rows[:], in_=k_view[b, g])
+            v_rows = loads.tile([P, PACK, D], BF16, name="v_rows")
+            nc.sync.dma_start(out=v_rows[:], in_=v_view[b, g])
+            key_loads[(b, g)] = (k_rows, v_rows)
+
+        def split_piece(piece):
+            b, rest = divmod(piece, PIECES_PER_BATCH)
+            g, part = divmod(rest, PIECES_PER_PASS)
+            return b, g, slice(part * PIECE, (part + 1) * PIECE)
+
+        def exp_keys(piece):
+            b, g, cols = split_piece(piece)
+            ek = stage.tile([P, PACK, PIECE], F32, name="ek")
+            nc.scalar.activation(out=ek[:], in_=key_loads[(b, g)][0][:, :, cols], func=ACT.Exp)
+            key_exp[piece] = ek
+
+        def quantise_keys(piece):
+            b, g, cols = split_piece(piece)
+            if b not in key_codes:
+                ek_codes = codes.tile([P, PASSES, D], U32, name="ek_codes", align_bytes=64)
+                ek_scales = codes.tile([P, PASSES, D], U8, name="ek_scales", align_bytes=64)
+                ekv_codes = codes.tile([P, PASSES, D], U32, name="ekv_codes", align_bytes=64)
+                ekv_scales = codes.tile([P, PASSES, D], U8, name="ekv_scales", align_bytes=64)
+                key_codes[b] = (ek_codes, ek_scales, ekv_codes, ekv_scales)
+            ek_codes, ek_scales, ekv_codes, ekv_scales = key_codes[b]
+            ek_by_column = key_exp[piece][:].rearrange("p t d -> p d t")
+            v_by_column = key_loads[(b, g)][1][:, :, cols].rearrange("p t d -> p d t")
+            ek_grouped = stage.tile([P, PIECE, PACK], BF16, name="ek_grouped", align_bytes=64)
+            nc.vector.tensor_copy(out=ek_grouped[:], in_=ek_by_column)
+            ekv_grouped = stage.tile([P, PIECE, PACK], BF16, name="ekv_grouped", align_bytes=64)
+            nc.vector.tensor_tensor(
+                out=ekv_grouped[:], in0=ek_by_column, in1=v_by_column, op=ALU.mult
+            )
+            nc.vector.quantize_mx(
+                out=ek_codes[:, g, cols].bitcast(FP8X4),
+                scales=ek_scales[:, g, cols],
+                in_=ek_grouped[:].rearrange("p d t -> p (d t)"),
+            )
+            nc.vector.quantize_mx(
+                out=ekv_codes[:, g, cols].bitcast(FP8X4),
+                scales=ekv_scales[:, g, cols],
+                in_=ekv_grouped[:].rearrange("p d t -> p (d t)"),
+            )
+
+        def form_exponents(t):
+            dist, mask = halves[t // LOAD_TILES][0:2]
+            row = t % LOAD_TILES
+            exponent = stage.tile([P, M], F32, name="exponent")
+            nc.vector.scalar_tensor_tensor(
+                out=exponent[:], in0=dist[:, row, :], scalar=neg_slope[:, 0:1],
+                in1=mask[:, row, :], op0=ALU.mult, op1=ALU.add,
+            )
+            exponents[t] = exponent
+
+        def project_and_transpose(t_q, t_next):
+            if is_tile(t_q):
+                b, i = divmod(t_q, TILES_PER_BATCH)
+                q_acc = psum_q.tile([P, D], F32, name="q_acc")
+                q_ps[t_q] = q_acc
+            if is_tile(t_next):
+                node = halves[t_next // LOAD_TILES][2]
+                row = t_next % LOAD_TILES
+                et = psum_et.tile([P, F_CHUNKS, P], BF16, name="et")
+                node_ps[t_next] = et
+                transposed[t_next] = []
+            for c in range(F_CHUNKS):
+                if is_tile(t_q):
+                    nc.tensor.matmul(
+                        out=q_acc[:], lhsT=node_t[t_q][:, c, :], rhs=wq_t[:, c, :],
+                        start=(c == 0), stop=False,
+                    )
+                if is_tile(t_next):
+                    for j in range(c * BLOCKS_PER_MATMUL, (c + 1) * BLOCKS_PER_MATMUL):
+                        if j % PACK == 0:
+                            xt = psum_xt.tile([P, PACK, P], F32, name="xt")
+                            transposed[t_next].append(xt)
+                        nc.tensor.transpose(
+                            xt[:, j % PACK, :], exponents[t_next][:, j * P : (j + 1) * P],
+                            ident_f32[:],
+                        )
+                    nc.tensor.transpose(
+                        et[:, c, :], node[:, row, c * P : (c + 1) * P], ident_bf16[:]
+                    )
+            if is_tile(t_q):
+                nc.tensor.matmul(
+                    out=q_acc[:], lhsT=load_by_tile[:, b, i, :], rhs=wq_t[:, F_CHUNKS, :],
+                    start=False, stop=True,
+                )
+
+        def exp_scores(t):
+            eb_grouped = stage.tile([P, PASSES, P, PACK], BF16, name="eb_grouped", align_bytes=64)
+            for g in range(PASSES):
+                nc.scalar.activation(
+                    out=eb_grouped[:, g, :, :],
+                    in_=transposed[t][g][:].rearrange("p t r -> p r t"),
+                    func=ACT.Exp,
+                )
+            scores[t] = eb_grouped
+
+        def quantise_scores(t):
+            b, i = divmod(t, TILES_PER_BATCH)
+            if b not in score_codes:
+                eb_codes = codes.tile(
+                    [P, TILES_PER_BATCH, PASSES, P], U32, name="eb_codes", align_bytes=64
+                )
+                eb_scales = codes.tile(
+                    [P, TILES_PER_BATCH, PASSES, P], U8, name="eb_scales", align_bytes=64
+                )
+                score_codes[b] = (eb_codes, eb_scales)
+            eb_codes, eb_scales = score_codes[b]
+            nc.vector.quantize_mx(
+                out=eb_codes[:, i, :, :].rearrange("p g r -> p (g r)").bitcast(FP8X4),
+                scales=eb_scales[:, i, :, :].rearrange("p g r -> p (g r)"),
+                in_=scores[t][:].rearrange("p g r t -> p (g r t)"),
+            )
+
+        def copy_node_t(t):
+            node_cols = stage.tile([P, F_CHUNKS, P], BF16, name="node_cols")
+            nc.vector.tensor_copy(out=node_cols[:], in_=node_ps[t][:])
+            node_t[t] = node_cols
+
+        def mix(t, which):
+            b, i = divmod(t, TILES_PER_BATCH)
+            eb_codes, eb_scales = score_codes[b]
+            acc = psum_acc.tile([P, D], F32, name="acc")
+            for g in range(PASSES):
+                nc.tensor.matmul_mx(
+                    out=acc[:],
+                    lhsT=eb_codes[:, i, g, :].bitcast(FP8X4),
+                    lhsT_scale=eb_scales[:, i, g, :],
+                    rhs=key_codes[b][which][:, g, :].bitcast(FP8X4),
+                    rhs_scale=key_codes[b][which + 1][:, g, :],
+                    start=(g == 0),
+                    stop=(g == PASSES - 1),
+                )
+            return acc
+
+        def tanh_gate(t):
+            gate_t = gates.tile([P, D], F32, name="gate_t")
+            nc.scalar.activation(out=gate_t[:], in_=q_ps[t][:], func=ACT.Tanh, scale=0.5)
+            gate[t] = gate_t
+
+        def merge_gate_and_num(t):
+            nc.vector.scalar_tensor_tensor(
+                out=gate[t][:], in0=gate[t][:], scalar=1.0, in1=num_ps[t][:],
+                op0=ALU.add, op1=ALU.mult,
+            )
+
+        def log_of_den(t):
+            den = mix(t, 0)
+            log_t = logs.tile([P, D], F32, name="log_t")
+            nc.scalar.activation(out=log_t[:], in_=den[:], func=ACT.Ln)
+            log_den[t] = log_t
+
+        def reciprocal_of_den(t):
+            nc.scalar.activation(out=log_den[t][:], in_=log_den[t][:], func=ACT.Exp, scale=-1.0)
+
+        def finish(t):
+            b, i = divmod(t, TILES_PER_BATCH)
+            nc.vector.scalar_tensor_tensor(
+                out=gate[t][:], in0=gate[t][:], scalar=0.5, in1=log_den[t][:],
+                op0=ALU.mult, op1=ALU.mult,
+            )
+            nc.sync.dma_start(out=out_view[b, :, i, :], in_=gate[t][:])
+
+        for step in range(FIRST_STEP, LAST_STEP + 1):
+            key_load, rest = divmod(step + KEY_LOAD_LEAD, PIECES_PER_PASS)
+            if rest == 0 and key_load < B * PASSES:
+                load_keys(key_load // PASSES, key_load % PASSES)
+            query_load, rest = divmod(step + LOAD_LEAD, LOAD_TILES)
+            if rest == 0 and 0 <= query_load < TILES // LOAD_TILES:
+                load_queries(query_load)
+
+            if is_tile(step + EXP_LEAD):
+                copy_node_t(step + EXP_LEAD)
+            if is_tile(step - MERGE_LAG):
+                merge_gate_and_num(step - MERGE_LAG)
+            if is_tile(step):
+                quantise_scores(step)
+            if is_tile(step + EXPONENT_LEAD):
+                form_exponents(step + EXPONENT_LEAD)
+            if is_piece(step + KEY_LEAD - 1):
+                quantise_keys(step + KEY_LEAD - 1)
+            if is_tile(step - FINISH_LAG):
+                finish(step - FINISH_LAG)
+
+            if is_tile(step - NUM_LAG):
+                num_ps[step - NUM_LAG] = mix(step - NUM_LAG, 2)
+            project_and_transpose(step, step + TRANSPOSE_LEAD)
+
+            if is_tile(step - NUM_LAG):
+                tanh_gate(step - NUM_LAG)
+            if is_tile(step + EXP_LEAD):
+                exp_scores(step + EXP_LEAD)
+            if is_piece(step + KEY_LEAD):
+                exp_keys(step + KEY_LEAD)
+            if is_tile(step - RECIP_LAG):
+                reciprocal_of_den(step - RECIP_LAG)
+
+            batch, rest = divmod(step - LN_LAG + 1, TILES_PER_BATCH)
+            if rest == 0 and 1 <= batch <= B:
+                for t in range((batch - 1) * TILES_PER_BATCH, batch * TILES_PER_BATCH):
+                    log_of_den(t)

@@ -22,7 +22,7 @@ TILES_PER_BATCH = N // P
 TILES = B * TILES_PER_BATCH
 LOAD_TILES = 4
 F_CHUNKS = D // P
-BLOCKS_PER_MATMUL = M // P // F_CHUNKS
+T_PER_MATMUL = (M // P + F_CHUNKS) // F_CHUNKS
 PIECE = P
 PIECES_PER_PASS = D // PIECE
 PIECES_PER_BATCH = PASSES * PIECES_PER_PASS
@@ -40,7 +40,7 @@ FINISH_LAG = RECIP_LAG + 1
 LOAD_LEAD = EXPONENT_LEAD + 3
 KEY_LEAD = PIECES_PER_BATCH
 KEY_LOAD_LEAD = KEY_LEAD + 3
-FIRST_STEP = -KEY_LOAD_LEAD
+FIRST_STEP = -LOAD_LEAD
 LAST_STEP = TILES - 1 + FINISH_LAG
 
 
@@ -62,50 +62,13 @@ def tile_cvrp_decoder_pa_t_kernel(
         loads = ctx.enter_context(tc.tile_pool(name="loads", bufs=2))
         codes = ctx.enter_context(tc.tile_pool(name="codes", bufs=2))
         stage = ctx.enter_context(tc.tile_pool(name="stage", bufs=3))
+        values = ctx.enter_context(tc.tile_pool(name="values", bufs=2 * PASSES))
+        grouped = ctx.enter_context(tc.tile_pool(name="grouped", bufs=PASSES))
         gates = ctx.enter_context(tc.tile_pool(name="gates", bufs=FINISH_LAG + 2))
         logs = ctx.enter_context(tc.tile_pool(name="logs", bufs=TILES_PER_BATCH + 2))
         psum_xt = ctx.enter_context(tc.psum_pool(name="psum_xt", bufs=3))
         psum_et = ctx.enter_context(tc.psum_pool(name="psum_et", bufs=1))
-        psum_q = ctx.enter_context(tc.psum_pool(name="psum_q", bufs=2))
-        psum_acc = ctx.enter_context(tc.psum_pool(name="psum_acc", bufs=2))
-
-        ident_f32 = consts.tile([P, P], F32, name="ident_f32")
-        make_identity(nc, ident_f32[:])
-        ident_bf16 = consts.tile([P, P], BF16, name="ident_bf16")
-        make_identity(nc, ident_bf16[:])
-
-        alpha_all = consts.tile([P, 1], BF16, name="alpha_all")
-        nc.sync.dma_start(out=alpha_all[:], in_=alpha1.partition_broadcast(P))
-        scale_all = consts.tile([P, 1], BF16, name="scale_all")
-        nc.sync.dma_start(out=scale_all[:], in_=log_scale.partition_broadcast(P))
-        neg_slope = consts.tile([P, 1], F32, name="neg_slope")
-        nc.vector.scalar_tensor_tensor(
-            out=neg_slope[:], in0=alpha_all[:], scalar=-1.0, in1=scale_all[:],
-            op0=ALU.mult, op1=ALU.mult,
-        )
-
-        load_rows = consts.tile([P, B * N], BF16, name="load_rows")
-        nc.vector.memset(load_rows[:], 0.0)
-        nc.sync.dma_start(
-            out=load_rows[P - 1 : P, :], in_=load.rearrange("(o b) n -> o (b n)", o=1)
-        )
-        load_by_tile = load_rows[:].rearrange(
-            "q (b p i) -> q b i p", b=B, i=TILES_PER_BATCH
-        )
-
-        wq_rows = consts.tile([P, F_CHUNKS, D + 2], BF16, name="wq_rows")
-        nc.sync.dma_start(
-            out=wq_rows[:, :, 0 : D + 1], in_=Wq_last.rearrange("(t p) f -> p t f", p=P)
-        )
-        wq_t = consts.tile([P, F_CHUNKS + 1, D], BF16, name="wq_t")
-        for c in range(F_CHUNKS + 1):
-            first = min(c * P, D + 1 - P)
-            et = psum_et.tile([P, F_CHUNKS, P], BF16, name="et")
-            for t in range(F_CHUNKS):
-                nc.tensor.transpose(et[:, t, :], wq_rows[:, t, first : first + P], ident_bf16[:])
-            nc.vector.tensor_copy(
-                out=wq_t[:, c, :], in_=et[:].rearrange("p t d -> p (t d)")
-            )
+        psum_out = ctx.enter_context(tc.psum_pool(name="psum_out", bufs=4))
 
         halves = {}
         key_loads = {}
@@ -125,9 +88,6 @@ def tile_cvrp_decoder_pa_t_kernel(
         def is_tile(t):
             return 0 <= t < TILES
 
-        def is_piece(piece):
-            return 0 <= piece < PIECES
-
         def load_queries(h):
             b, first = divmod(h * LOAD_TILES, TILES_PER_BATCH)
             rows = slice(first, first + LOAD_TILES)
@@ -142,48 +102,50 @@ def tile_cvrp_decoder_pa_t_kernel(
         def load_keys(b, g):
             k_rows = loads.tile([P, PACK, D], BF16, name="k_rows")
             nc.sync.dma_start(out=k_rows[:], in_=k_view[b, g])
-            v_rows = loads.tile([P, PACK, D], BF16, name="v_rows")
+            v_rows = values.tile([P, PACK, D], BF16, name="v_rows")
             nc.sync.dma_start(out=v_rows[:], in_=v_view[b, g])
             key_loads[(b, g)] = (k_rows, v_rows)
 
-        def split_piece(piece):
+        def exp_keys(piece):
             b, rest = divmod(piece, PIECES_PER_BATCH)
             g, part = divmod(rest, PIECES_PER_PASS)
-            return b, g, slice(part * PIECE, (part + 1) * PIECE)
+            if part == 0:
+                ek = stage.tile([P, PACK, D], F32, name="ek")
+                key_exp[(b, g)] = ek
+            cols = slice(part * PIECE, (part + 1) * PIECE)
+            nc.scalar.activation(
+                out=key_exp[(b, g)][:, :, cols], in_=key_loads[(b, g)][0][:, :, cols], func=ACT.Exp
+            )
 
-        def exp_keys(piece):
-            b, g, cols = split_piece(piece)
-            ek = stage.tile([P, PACK, PIECE], F32, name="ek")
-            nc.scalar.activation(out=ek[:], in_=key_loads[(b, g)][0][:, :, cols], func=ACT.Exp)
-            key_exp[piece] = ek
-
-        def quantise_keys(piece):
-            b, g, cols = split_piece(piece)
-            if b not in key_codes:
-                ek_codes = codes.tile([P, PASSES, D], U32, name="ek_codes", align_bytes=64)
-                ek_scales = codes.tile([P, PASSES, D], U8, name="ek_scales", align_bytes=64)
-                ekv_codes = codes.tile([P, PASSES, D], U32, name="ekv_codes", align_bytes=64)
-                ekv_scales = codes.tile([P, PASSES, D], U8, name="ekv_scales", align_bytes=64)
-                key_codes[b] = (ek_codes, ek_scales, ekv_codes, ekv_scales)
-            ek_codes, ek_scales, ekv_codes, ekv_scales = key_codes[b]
-            ek_by_column = key_exp[piece][:].rearrange("p t d -> p d t")
-            v_by_column = key_loads[(b, g)][1][:, :, cols].rearrange("p t d -> p d t")
-            ek_grouped = stage.tile([P, PIECE, PACK], BF16, name="ek_grouped", align_bytes=64)
-            nc.vector.tensor_copy(out=ek_grouped[:], in_=ek_by_column)
-            ekv_grouped = stage.tile([P, PIECE, PACK], BF16, name="ekv_grouped", align_bytes=64)
-            nc.vector.tensor_tensor(
-                out=ekv_grouped[:], in0=ek_by_column, in1=v_by_column, op=ALU.mult
-            )
-            nc.vector.quantize_mx(
-                out=ek_codes[:, g, cols].bitcast(FP8X4),
-                scales=ek_scales[:, g, cols],
-                in_=ek_grouped[:].rearrange("p d t -> p (d t)"),
-            )
-            nc.vector.quantize_mx(
-                out=ekv_codes[:, g, cols].bitcast(FP8X4),
-                scales=ekv_scales[:, g, cols],
-                in_=ekv_grouped[:].rearrange("p d t -> p (d t)"),
-            )
+        def quantise_keys(b):
+            ek_codes = codes.tile([P, PASSES, D], U32, name="ek_codes", align_bytes=64)
+            ek_scales = codes.tile([P, PASSES, D], U8, name="ek_scales", align_bytes=64)
+            ekv_codes = codes.tile([P, PASSES, D], U32, name="ekv_codes", align_bytes=64)
+            ekv_scales = codes.tile([P, PASSES, D], U8, name="ekv_scales", align_bytes=64)
+            key_codes[b] = (ek_codes, ek_scales, ekv_codes, ekv_scales)
+            rounded = []
+            for g in range(PASSES):
+                ek_by_column = key_exp[(b, g)][:].rearrange("p t d -> p d t")
+                v_by_column = key_loads[(b, g)][1][:].rearrange("p t d -> p d t")
+                ek_grouped = grouped.tile([P, D, PACK], BF16, name="ek_grouped", align_bytes=64)
+                nc.vector.tensor_copy(out=ek_grouped[:], in_=ek_by_column)
+                ekv_grouped = grouped.tile([P, D, PACK], BF16, name="ekv_grouped", align_bytes=64)
+                nc.vector.tensor_tensor(
+                    out=ekv_grouped[:], in0=ek_by_column, in1=v_by_column, op=ALU.mult
+                )
+                rounded.append((ek_grouped, ekv_grouped))
+            for g in range(PASSES):
+                ek_grouped, ekv_grouped = rounded[g]
+                nc.vector.quantize_mx(
+                    out=ek_codes[:, g, :].bitcast(FP8X4),
+                    scales=ek_scales[:, g, :],
+                    in_=ek_grouped[:].rearrange("p d t -> p (d t)"),
+                )
+                nc.vector.quantize_mx(
+                    out=ekv_codes[:, g, :].bitcast(FP8X4),
+                    scales=ekv_scales[:, g, :],
+                    in_=ekv_grouped[:].rearrange("p d t -> p (d t)"),
+                )
 
         def form_exponents(t):
             dist, mask = halves[t // LOAD_TILES][0:2]
@@ -195,35 +157,48 @@ def tile_cvrp_decoder_pa_t_kernel(
             )
             exponents[t] = exponent
 
+        def transposes_for(t):
+            node = halves[t // LOAD_TILES][2]
+            row = t % LOAD_TILES
+            xts = []
+            for g in range(PASSES):
+                xt = psum_xt.tile([P, PACK, P], F32, name="xt")
+                xts.append(xt)
+            et = psum_et.tile([P, F_CHUNKS, P], BF16, name="et")
+            transposed[t] = xts
+            node_ps[t] = et
+
+            def exponent_block(g, j):
+                first = (g * PACK + j) * P
+                return lambda: nc.tensor.transpose(
+                    xts[g][:, j, :], exponents[t][:, first : first + P], ident_f32[:]
+                )
+
+            def node_block(c):
+                return lambda: nc.tensor.transpose(
+                    et[:, c, :], node[:, row, c * P : (c + 1) * P], ident_bf16[:]
+                )
+
+            return (
+                [exponent_block(0, j) for j in range(PACK)]
+                + [node_block(c) for c in range(F_CHUNKS)]
+                + [exponent_block(1, j) for j in range(PACK)]
+            )
+
         def project_and_transpose(t_q, t_next):
+            waiting = transposes_for(t_next) if is_tile(t_next) else []
             if is_tile(t_q):
                 b, i = divmod(t_q, TILES_PER_BATCH)
-                q_acc = psum_q.tile([P, D], F32, name="q_acc")
+                q_acc = psum_out.tile([P, D], F32, name="q_acc", tag="out_bank")
                 q_ps[t_q] = q_acc
-            if is_tile(t_next):
-                node = halves[t_next // LOAD_TILES][2]
-                row = t_next % LOAD_TILES
-                et = psum_et.tile([P, F_CHUNKS, P], BF16, name="et")
-                node_ps[t_next] = et
-                transposed[t_next] = []
             for c in range(F_CHUNKS):
                 if is_tile(t_q):
                     nc.tensor.matmul(
                         out=q_acc[:], lhsT=node_t[t_q][:, c, :], rhs=wq_t[:, c, :],
                         start=(c == 0), stop=False,
                     )
-                if is_tile(t_next):
-                    for j in range(c * BLOCKS_PER_MATMUL, (c + 1) * BLOCKS_PER_MATMUL):
-                        if j % PACK == 0:
-                            xt = psum_xt.tile([P, PACK, P], F32, name="xt")
-                            transposed[t_next].append(xt)
-                        nc.tensor.transpose(
-                            xt[:, j % PACK, :], exponents[t_next][:, j * P : (j + 1) * P],
-                            ident_f32[:],
-                        )
-                    nc.tensor.transpose(
-                        et[:, c, :], node[:, row, c * P : (c + 1) * P], ident_bf16[:]
-                    )
+                for transpose_block in waiting[c * T_PER_MATMUL : (c + 1) * T_PER_MATMUL]:
+                    transpose_block()
             if is_tile(t_q):
                 nc.tensor.matmul(
                     out=q_acc[:], lhsT=load_by_tile[:, b, i, :], rhs=wq_t[:, F_CHUNKS, :],
@@ -265,7 +240,7 @@ def tile_cvrp_decoder_pa_t_kernel(
         def mix(t, which):
             b, i = divmod(t, TILES_PER_BATCH)
             eb_codes, eb_scales = score_codes[b]
-            acc = psum_acc.tile([P, D], F32, name="acc")
+            acc = psum_out.tile([P, D], F32, name="acc", tag="out_bank")
             for g in range(PASSES):
                 nc.tensor.matmul_mx(
                     out=acc[:],
@@ -306,12 +281,55 @@ def tile_cvrp_decoder_pa_t_kernel(
             )
             nc.sync.dma_start(out=out_view[b, :, i, :], in_=gate[t][:])
 
+        load_rows = consts.tile([P, B * N], BF16, name="load_rows")
+        nc.vector.memset(load_rows[:], 0.0)
+
+        alpha_all = consts.tile([P, 1], BF16, name="alpha_all")
+        nc.sync.dma_start(out=alpha_all[:], in_=alpha1.partition_broadcast(P))
+        scale_all = consts.tile([P, 1], BF16, name="scale_all")
+        nc.sync.dma_start(out=scale_all[:], in_=log_scale.partition_broadcast(P))
+        for g in range(PASSES):
+            load_keys(0, g)
+        neg_slope = consts.tile([P, 1], F32, name="neg_slope")
+        nc.vector.scalar_tensor_tensor(
+            out=neg_slope[:], in0=alpha_all[:], scalar=-1.0, in1=scale_all[:],
+            op0=ALU.mult, op1=ALU.mult,
+        )
+
+        wq_rows = consts.tile([P, F_CHUNKS, D + 2], BF16, name="wq_rows")
+        nc.sync.dma_start(
+            out=wq_rows[:, :, 0 : D + 1], in_=Wq_last.rearrange("(t p) f -> p t f", p=P)
+        )
+        nc.sync.dma_start(
+            out=load_rows[P - 1 : P, :], in_=load.rearrange("(o b) n -> o (b n)", o=1)
+        )
+        load_by_tile = load_rows[:].rearrange("q (b p i) -> q b i p", b=B, i=TILES_PER_BATCH)
+
+        ident_f32 = consts.tile([P, P], F32, name="ident_f32")
+        make_identity(nc, ident_f32[:])
+        ident_bf16 = consts.tile([P, P], BF16, name="ident_bf16")
+        make_identity(nc, ident_bf16[:])
+
+        for piece in range(PIECES_PER_BATCH):
+            exp_keys(piece)
+        quantise_keys(0)
+
+        wq_t = consts.tile([P, F_CHUNKS + 1, D], BF16, name="wq_t")
+        for c in range(F_CHUNKS + 1):
+            first = min(c * P, D + 1 - P)
+            wq_ps = psum_out.tile([P, F_CHUNKS, P], BF16, name="wq_ps", tag="out_bank")
+            for t in range(F_CHUNKS):
+                nc.tensor.transpose(
+                    wq_ps[:, t, :], wq_rows[:, t, first : first + P], ident_bf16[:]
+                )
+            nc.vector.tensor_copy(out=wq_t[:, c, :], in_=wq_ps[:].rearrange("p t d -> p (t d)"))
+
         for step in range(FIRST_STEP, LAST_STEP + 1):
             key_load, rest = divmod(step + KEY_LOAD_LEAD, PIECES_PER_PASS)
-            if rest == 0 and key_load < B * PASSES:
+            if rest == 0 and PASSES <= key_load < B * PASSES:
                 load_keys(key_load // PASSES, key_load % PASSES)
             query_load, rest = divmod(step + LOAD_LEAD, LOAD_TILES)
-            if rest == 0 and 0 <= query_load < TILES // LOAD_TILES:
+            if rest == 0 and query_load < TILES // LOAD_TILES:
                 load_queries(query_load)
 
             if is_tile(step + EXP_LEAD):
@@ -322,20 +340,21 @@ def tile_cvrp_decoder_pa_t_kernel(
                 quantise_scores(step)
             if is_tile(step + EXPONENT_LEAD):
                 form_exponents(step + EXPONENT_LEAD)
-            if is_piece(step + KEY_LEAD - 1):
-                quantise_keys(step + KEY_LEAD - 1)
+            batch, rest = divmod(step - LN_LAG, TILES_PER_BATCH)
+            if rest == 0 and 1 <= batch < B:
+                quantise_keys(batch)
             if is_tile(step - FINISH_LAG):
                 finish(step - FINISH_LAG)
 
+            project_and_transpose(step, step + TRANSPOSE_LEAD)
             if is_tile(step - NUM_LAG):
                 num_ps[step - NUM_LAG] = mix(step - NUM_LAG, 2)
-            project_and_transpose(step, step + TRANSPOSE_LEAD)
 
-            if is_tile(step - NUM_LAG):
-                tanh_gate(step - NUM_LAG)
             if is_tile(step + EXP_LEAD):
                 exp_scores(step + EXP_LEAD)
-            if is_piece(step + KEY_LEAD):
+            if is_tile(step - NUM_LAG):
+                tanh_gate(step - NUM_LAG)
+            if PIECES_PER_BATCH <= step + KEY_LEAD < PIECES:
                 exp_keys(step + KEY_LEAD)
             if is_tile(step - RECIP_LAG):
                 reciprocal_of_den(step - RECIP_LAG)

@@ -24,6 +24,7 @@ LOAD_TILES = 4
 F_CHUNKS = D // P
 T_PER_MATMUL = (M // P + F_CHUNKS) // F_CHUNKS
 PIECE = P
+RUN = 4
 PIECES_PER_PASS = D // PIECE
 PIECES_PER_BATCH = PASSES * PIECES_PER_PASS
 PIECES = B * PIECES_PER_BATCH
@@ -125,13 +126,16 @@ def tile_cvrp_decoder_pa_t_kernel(
             key_codes[b] = (ek_codes, ek_scales, ekv_codes, ekv_scales)
             rounded = []
             for g in range(PASSES):
-                ek_by_column = key_exp[(b, g)][:].rearrange("p t d -> p d t")
-                v_by_column = key_loads[(b, g)][1][:].rearrange("p t d -> p d t")
+                ek_runs = key_exp[(b, g)][:].rearrange("p t (c i) -> p c t i", i=RUN)
+                v_runs = key_loads[(b, g)][1][:].rearrange("p t (c i) -> p c t i", i=RUN)
                 ek_grouped = grouped.tile([P, D, PACK], BF16, name="ek_grouped", align_bytes=64)
-                nc.vector.tensor_copy(out=ek_grouped[:], in_=ek_by_column)
+                nc.vector.tensor_copy(
+                    out=ek_grouped[:].rearrange("p (c i) t -> p c t i", i=RUN), in_=ek_runs
+                )
                 ekv_grouped = grouped.tile([P, D, PACK], BF16, name="ekv_grouped", align_bytes=64)
                 nc.vector.tensor_tensor(
-                    out=ekv_grouped[:], in0=ek_by_column, in1=v_by_column, op=ALU.mult
+                    out=ekv_grouped[:].rearrange("p (c i) t -> p c t i", i=RUN),
+                    in0=ek_runs, in1=v_runs, op=ALU.mult,
                 )
                 rounded.append((ek_grouped, ekv_grouped))
             for g in range(PASSES):

@@ -20,15 +20,15 @@ K_PASS = P * PACK
 PASSES = M // K_PASS
 TILES_PER_BATCH = N // P
 TILES = B * TILES_PER_BATCH
-LOAD_TILES = 4
+LOAD_TILES = TILES_PER_BATCH // 2
 F_CHUNKS = D // P
 T_PER_MATMUL = (M // P + F_CHUNKS) // F_CHUNKS
 PIECE = P
-RUN = 4
 PIECES_PER_PASS = D // PIECE
 PIECES_PER_BATCH = PASSES * PIECES_PER_PASS
 PIECES = B * PIECES_PER_BATCH
 assert PIECES_PER_BATCH == TILES_PER_BATCH
+RUN = 4
 
 EXPONENT_LEAD = 3
 TRANSPOSE_LEAD = 2
@@ -38,9 +38,10 @@ MERGE_LAG = 2
 LN_LAG = 1
 RECIP_LAG = TILES_PER_BATCH + LN_LAG
 FINISH_LAG = RECIP_LAG + 1
-LOAD_LEAD = EXPONENT_LEAD + 3
+DMA_STEPS = 3
+LOAD_LEAD = EXPONENT_LEAD + DMA_STEPS
 KEY_LEAD = PIECES_PER_BATCH
-KEY_LOAD_LEAD = KEY_LEAD + 3
+KEY_LOAD_LEAD = KEY_LEAD + DMA_STEPS
 FIRST_STEP = -LOAD_LEAD
 LAST_STEP = TILES - 1 + FINISH_LAG
 
@@ -54,16 +55,16 @@ def tile_cvrp_decoder_pa_t_kernel(
     mask_view = ninf_mask.rearrange("b (p i) m -> b p i m", i=TILES_PER_BATCH)
     node_view = encoded_last_node.rearrange("b (p i) f -> b p i f", i=TILES_PER_BATCH)
     out_view = out.rearrange("b (p i) d -> b p i d", i=TILES_PER_BATCH)
-    k_view = k.rearrange("b (g t p) d -> b g p t d", g=PASSES, t=PACK)
-    v_view = v.rearrange("b (g t p) d -> b g p t d", g=PASSES, t=PACK)
+    k_view = k.rearrange("b (g j p) d -> b g p j d", g=PASSES, j=PACK)
+    v_view = v.rearrange("b (g j p) d -> b g p j d", g=PASSES, j=PACK)
 
     with ExitStack() as ctx:
         ctx.enter_context(tc.manual_schedule())
         consts = ctx.enter_context(tc.tile_pool(name="consts", bufs=1))
         loads = ctx.enter_context(tc.tile_pool(name="loads", bufs=2))
+        values = ctx.enter_context(tc.tile_pool(name="values", bufs=2 * PASSES))
         codes = ctx.enter_context(tc.tile_pool(name="codes", bufs=2))
         stage = ctx.enter_context(tc.tile_pool(name="stage", bufs=3))
-        values = ctx.enter_context(tc.tile_pool(name="values", bufs=2 * PASSES))
         grouped = ctx.enter_context(tc.tile_pool(name="grouped", bufs=PASSES))
         gates = ctx.enter_context(tc.tile_pool(name="gates", bufs=FINISH_LAG + 2))
         logs = ctx.enter_context(tc.tile_pool(name="logs", bufs=TILES_PER_BATCH + 2))
@@ -71,7 +72,7 @@ def tile_cvrp_decoder_pa_t_kernel(
         psum_et = ctx.enter_context(tc.psum_pool(name="psum_et", bufs=1))
         psum_out = ctx.enter_context(tc.psum_pool(name="psum_out", bufs=4))
 
-        halves = {}
+        query_loads = {}
         key_loads = {}
         key_exp = {}
         key_codes = {}
@@ -98,7 +99,7 @@ def tile_cvrp_decoder_pa_t_kernel(
             nc.sync.dma_start(out=mask[:], in_=mask_view[b, :, rows, :])
             node = loads.tile([P, LOAD_TILES, D], BF16, name="node")
             nc.sync.dma_start(out=node[:], in_=node_view[b, :, rows, :])
-            halves[h] = (dist, mask, node)
+            query_loads[h] = (dist, mask, node)
 
         def load_keys(b, g):
             k_rows = loads.tile([P, PACK, D], BF16, name="k_rows")
@@ -118,41 +119,30 @@ def tile_cvrp_decoder_pa_t_kernel(
                 out=key_exp[(b, g)][:, :, cols], in_=key_loads[(b, g)][0][:, :, cols], func=ACT.Exp
             )
 
-        def quantise_keys(b):
-            ek_codes = codes.tile([P, PASSES, D], U32, name="ek_codes", align_bytes=64)
-            ek_scales = codes.tile([P, PASSES, D], U8, name="ek_scales", align_bytes=64)
-            ekv_codes = codes.tile([P, PASSES, D], U32, name="ekv_codes", align_bytes=64)
-            ekv_scales = codes.tile([P, PASSES, D], U8, name="ekv_scales", align_bytes=64)
-            key_codes[b] = (ek_codes, ek_scales, ekv_codes, ekv_scales)
+        def quantise_keys(b, kind):
+            words = codes.tile([P, PASSES, D], U32, name="%s_words" % kind, align_bytes=64)
+            scales = codes.tile([P, PASSES, D], U8, name="%s_scales" % kind, align_bytes=64)
+            key_codes[(b, kind)] = (words, scales)
             rounded = []
             for g in range(PASSES):
-                ek_runs = key_exp[(b, g)][:].rearrange("p t (c i) -> p c t i", i=RUN)
-                v_runs = key_loads[(b, g)][1][:].rearrange("p t (c i) -> p c t i", i=RUN)
-                ek_grouped = grouped.tile([P, D, PACK], BF16, name="ek_grouped", align_bytes=64)
-                nc.vector.tensor_copy(
-                    out=ek_grouped[:].rearrange("p (c i) t -> p c t i", i=RUN), in_=ek_runs
-                )
-                ekv_grouped = grouped.tile([P, D, PACK], BF16, name="ekv_grouped", align_bytes=64)
-                nc.vector.tensor_tensor(
-                    out=ekv_grouped[:].rearrange("p (c i) t -> p c t i", i=RUN),
-                    in0=ek_runs, in1=v_runs, op=ALU.mult,
-                )
-                rounded.append((ek_grouped, ekv_grouped))
+                in_order = grouped.tile([P, D, PACK], BF16, name="%s_in_order" % kind, align_bytes=64)
+                out_runs = in_order[:].rearrange("p (a e) j -> p a j e", e=RUN)
+                ek_runs = key_exp[(b, g)][:].rearrange("p j (a e) -> p a j e", e=RUN)
+                if kind == "ekv":
+                    v_runs = key_loads[(b, g)][1][:].rearrange("p j (a e) -> p a j e", e=RUN)
+                    nc.vector.tensor_tensor(out=out_runs, in0=ek_runs, in1=v_runs, op=ALU.mult)
+                else:
+                    nc.vector.tensor_copy(out=out_runs, in_=ek_runs)
+                rounded.append(in_order)
             for g in range(PASSES):
-                ek_grouped, ekv_grouped = rounded[g]
                 nc.vector.quantize_mx(
-                    out=ek_codes[:, g, :].bitcast(FP8X4),
-                    scales=ek_scales[:, g, :],
-                    in_=ek_grouped[:].rearrange("p d t -> p (d t)"),
-                )
-                nc.vector.quantize_mx(
-                    out=ekv_codes[:, g, :].bitcast(FP8X4),
-                    scales=ekv_scales[:, g, :],
-                    in_=ekv_grouped[:].rearrange("p d t -> p (d t)"),
+                    out=words[:, g, :].bitcast(FP8X4),
+                    scales=scales[:, g, :],
+                    in_=rounded[g][:].rearrange("p d j -> p (d j)"),
                 )
 
         def form_exponents(t):
-            dist, mask = halves[t // LOAD_TILES][0:2]
+            dist, mask = query_loads[t // LOAD_TILES][0:2]
             row = t % LOAD_TILES
             exponent = stage.tile([P, M], F32, name="exponent")
             nc.vector.scalar_tensor_tensor(
@@ -162,7 +152,7 @@ def tile_cvrp_decoder_pa_t_kernel(
             exponents[t] = exponent
 
         def transposes_for(t):
-            node = halves[t // LOAD_TILES][2]
+            node = query_loads[t // LOAD_TILES][2]
             row = t % LOAD_TILES
             xts = []
             for g in range(PASSES):
@@ -214,7 +204,7 @@ def tile_cvrp_decoder_pa_t_kernel(
             for g in range(PASSES):
                 nc.scalar.activation(
                     out=eb_grouped[:, g, :, :],
-                    in_=transposed[t][g][:].rearrange("p t r -> p r t"),
+                    in_=transposed[t][g][:].rearrange("p j r -> p r j"),
                     func=ACT.Exp,
                 )
             scores[t] = eb_grouped
@@ -233,7 +223,7 @@ def tile_cvrp_decoder_pa_t_kernel(
             nc.vector.quantize_mx(
                 out=eb_codes[:, i, :, :].rearrange("p g r -> p (g r)").bitcast(FP8X4),
                 scales=eb_scales[:, i, :, :].rearrange("p g r -> p (g r)"),
-                in_=scores[t][:].rearrange("p g r t -> p (g r t)"),
+                in_=scores[t][:].rearrange("p g r j -> p (g r j)"),
             )
 
         def copy_node_t(t):
@@ -241,17 +231,18 @@ def tile_cvrp_decoder_pa_t_kernel(
             nc.vector.tensor_copy(out=node_cols[:], in_=node_ps[t][:])
             node_t[t] = node_cols
 
-        def mix(t, which):
+        def mix(t, kind):
             b, i = divmod(t, TILES_PER_BATCH)
             eb_codes, eb_scales = score_codes[b]
+            key_words, key_scales = key_codes[(b, kind)]
             acc = psum_out.tile([P, D], F32, name="acc", tag="out_bank")
             for g in range(PASSES):
                 nc.tensor.matmul_mx(
                     out=acc[:],
                     lhsT=eb_codes[:, i, g, :].bitcast(FP8X4),
                     lhsT_scale=eb_scales[:, i, g, :],
-                    rhs=key_codes[b][which][:, g, :].bitcast(FP8X4),
-                    rhs_scale=key_codes[b][which + 1][:, g, :],
+                    rhs=key_words[:, g, :].bitcast(FP8X4),
+                    rhs_scale=key_scales[:, g, :],
                     start=(g == 0),
                     stop=(g == PASSES - 1),
                 )
@@ -269,7 +260,7 @@ def tile_cvrp_decoder_pa_t_kernel(
             )
 
         def log_of_den(t):
-            den = mix(t, 0)
+            den = mix(t, "ek")
             log_t = logs.tile([P, D], F32, name="log_t")
             nc.scalar.activation(out=log_t[:], in_=den[:], func=ACT.Ln)
             log_den[t] = log_t
@@ -302,7 +293,7 @@ def tile_cvrp_decoder_pa_t_kernel(
 
         wq_rows = consts.tile([P, F_CHUNKS, D + 2], BF16, name="wq_rows")
         nc.sync.dma_start(
-            out=wq_rows[:, :, 0 : D + 1], in_=Wq_last.rearrange("(t p) f -> p t f", p=P)
+            out=wq_rows[:, :, 0 : D + 1], in_=Wq_last.rearrange("(r p) f -> p r f", p=P)
         )
         nc.sync.dma_start(
             out=load_rows[P - 1 : P, :], in_=load.rearrange("(o b) n -> o (b n)", o=1)
@@ -316,17 +307,18 @@ def tile_cvrp_decoder_pa_t_kernel(
 
         for piece in range(PIECES_PER_BATCH):
             exp_keys(piece)
-        quantise_keys(0)
+        quantise_keys(0, "ekv")
+        quantise_keys(0, "ek")
 
         wq_t = consts.tile([P, F_CHUNKS + 1, D], BF16, name="wq_t")
         for c in range(F_CHUNKS + 1):
             first = min(c * P, D + 1 - P)
             wq_ps = psum_out.tile([P, F_CHUNKS, P], BF16, name="wq_ps", tag="out_bank")
-            for t in range(F_CHUNKS):
+            for r in range(F_CHUNKS):
                 nc.tensor.transpose(
-                    wq_ps[:, t, :], wq_rows[:, t, first : first + P], ident_bf16[:]
+                    wq_ps[:, r, :], wq_rows[:, r, first : first + P], ident_bf16[:]
                 )
-            nc.vector.tensor_copy(out=wq_t[:, c, :], in_=wq_ps[:].rearrange("p t d -> p (t d)"))
+            nc.scalar.copy(out=wq_t[:, c, :], in_=wq_ps[:].rearrange("p r d -> p (r d)"))
 
         for step in range(FIRST_STEP, LAST_STEP + 1):
             key_load, rest = divmod(step + KEY_LOAD_LEAD, PIECES_PER_PASS)
@@ -346,13 +338,14 @@ def tile_cvrp_decoder_pa_t_kernel(
                 form_exponents(step + EXPONENT_LEAD)
             batch, rest = divmod(step - LN_LAG, TILES_PER_BATCH)
             if rest == 0 and 1 <= batch < B:
-                quantise_keys(batch)
+                quantise_keys(batch, "ekv")
+                quantise_keys(batch, "ek")
             if is_tile(step - FINISH_LAG):
                 finish(step - FINISH_LAG)
 
             project_and_transpose(step, step + TRANSPOSE_LEAD)
             if is_tile(step - NUM_LAG):
-                num_ps[step - NUM_LAG] = mix(step - NUM_LAG, 2)
+                num_ps[step - NUM_LAG] = mix(step - NUM_LAG, "ekv")
 
             if is_tile(step + EXP_LEAD):
                 exp_scores(step + EXP_LEAD)

@@ -35,8 +35,7 @@ TRANSPOSE_LEAD = 2
 EXP_LEAD = 1
 NUM_LAG = 1
 MERGE_LAG = 2
-LN_LAG = 1
-RECIP_LAG = TILES_PER_BATCH + LN_LAG
+RECIP_LAG = TILES_PER_BATCH
 FINISH_LAG = RECIP_LAG + 1
 DMA_STEPS = 3
 LOAD_LEAD = EXPONENT_LEAD + DMA_STEPS
@@ -131,6 +130,8 @@ def tile_cvrp_decoder_pa_t_kernel(
                 if kind == "ekv":
                     v_runs = key_loads[(b, g)][1][:].rearrange("p j (a e) -> p a j e", e=RUN)
                     nc.vector.tensor_tensor(out=out_runs, in0=ek_runs, in1=v_runs, op=ALU.mult)
+                elif b == 0:
+                    nc.scalar.copy(out=out_runs, in_=ek_runs)
                 else:
                     nc.vector.tensor_copy(out=out_runs, in_=ek_runs)
                 rounded.append(in_order)
@@ -226,9 +227,9 @@ def tile_cvrp_decoder_pa_t_kernel(
                 in_=scores[t][:].rearrange("p g r j -> p (g r j)"),
             )
 
-        def copy_node_t(t):
+        def copy_node_t(t, copy):
             node_cols = stage.tile([P, F_CHUNKS, P], BF16, name="node_cols")
-            nc.vector.tensor_copy(out=node_cols[:], in_=node_ps[t][:])
+            copy(out=node_cols[:], in_=node_ps[t][:])
             node_t[t] = node_cols
 
         def mix(t, kind):
@@ -328,15 +329,15 @@ def tile_cvrp_decoder_pa_t_kernel(
             if rest == 0 and query_load < TILES // LOAD_TILES:
                 load_queries(query_load)
 
-            if is_tile(step + EXP_LEAD):
-                copy_node_t(step + EXP_LEAD)
+            if is_tile(step + EXP_LEAD) and (step + EXP_LEAD) % 2 == 1:
+                copy_node_t(step + EXP_LEAD, nc.vector.tensor_copy)
             if is_tile(step - MERGE_LAG):
                 merge_gate_and_num(step - MERGE_LAG)
             if is_tile(step):
                 quantise_scores(step)
             if is_tile(step + EXPONENT_LEAD):
                 form_exponents(step + EXPONENT_LEAD)
-            batch, rest = divmod(step - LN_LAG, TILES_PER_BATCH)
+            batch, rest = divmod(step, TILES_PER_BATCH)
             if rest == 0 and 1 <= batch < B:
                 quantise_keys(batch, "ekv")
                 quantise_keys(batch, "ek")
@@ -347,6 +348,8 @@ def tile_cvrp_decoder_pa_t_kernel(
             if is_tile(step - NUM_LAG):
                 num_ps[step - NUM_LAG] = mix(step - NUM_LAG, "ekv")
 
+            if is_tile(step + EXP_LEAD) and (step + EXP_LEAD) % 2 == 0:
+                copy_node_t(step + EXP_LEAD, nc.scalar.copy)
             if is_tile(step + EXP_LEAD):
                 exp_scores(step + EXP_LEAD)
             if is_tile(step - NUM_LAG):
@@ -356,7 +359,7 @@ def tile_cvrp_decoder_pa_t_kernel(
             if is_tile(step - RECIP_LAG):
                 reciprocal_of_den(step - RECIP_LAG)
 
-            batch, rest = divmod(step - LN_LAG + 1, TILES_PER_BATCH)
+            batch, rest = divmod(step + 1, TILES_PER_BATCH)
             if rest == 0 and 1 <= batch <= B:
                 for t in range((batch - 1) * TILES_PER_BATCH, batch * TILES_PER_BATCH):
                     log_of_den(t)

from contextlib import ExitStack

import concourse.mybir as mybir
from concourse.masks import make_identity

F32 = mybir.dt.float32
BF16 = mybir.dt.bfloat16
U32 = mybir.dt.uint32
U8 = mybir.dt.uint8
FP8X4 = mybir.dt.float8_e4m3fn_x4
ACT = mybir.ActivationFunctionType
ALU = mybir.AluOpType

B, N, M, D = 4, 1024, 1024, 512
FLOPS = 2 * B * N * D * (D + 1) + 2 * 2 * B * N * M * D

P = 128
PACK = 4
K_PASS = P * PACK
PASSES = M // K_PASS
TILES_PER_BATCH = N // P
TILES = B * TILES_PER_BATCH
LOAD_TILES = TILES_PER_BATCH // 2
F_CHUNKS = D // P
T_PER_MATMUL = (M // P + F_CHUNKS) // F_CHUNKS
PIECE = P
PIECES_PER_PASS = D // PIECE
PIECES_PER_BATCH = PASSES * PIECES_PER_PASS
PIECES = B * PIECES_PER_BATCH
assert PIECES_PER_BATCH == TILES_PER_BATCH
RUN = 4

EXPONENT_LEAD = 3
TRANSPOSE_LEAD = 2
EXP_LEAD = 1
NUM_LAG = 1
MERGE_LAG = 2
RECIP_LAG = TILES_PER_BATCH
FINISH_LAG = RECIP_LAG + 1
DMA_STEPS = 3
LOAD_LEAD = EXPONENT_LEAD + DMA_STEPS
KEY_LEAD = PIECES_PER_BATCH
KEY_LOAD_LEAD = KEY_LEAD + DMA_STEPS
FIRST_STEP = -LOAD_LEAD
LAST_STEP = TILES - 1 + FINISH_LAG


def tile_cvrp_decoder_pa_t_kernel(
    tc, encoded_last_node, load, cur_dist, log_scale, ninf_mask, k, v, Wq_last, alpha1, out
):
    nc = tc.nc

    dist_view = cur_dist.rearrange("b (p i) m -> b p i m", i=TILES_PER_BATCH)
    mask_view = ninf_mask.rearrange("b (p i) m -> b p i m", i=TILES_PER_BATCH)
    node_view = encoded_last_node.rearrange("b (p i) f -> b p i f", i=TILES_PER_BATCH)
    out_view = out.rearrange("b (p i) d -> b p i d", i=TILES_PER_BATCH)
    k_view = k.rearrange("b (g j p) d -> b g p j d", g=PASSES, j=PACK)
    v_view = v.rearrange("b (g j p) d -> b g p j d", g=PASSES, j=PACK)

    with ExitStack() as ctx:
        ctx.enter_context(tc.manual_schedule())
        consts = ctx.enter_context(tc.tile_pool(name="consts", bufs=1))
        loads = ctx.enter_context(tc.tile_pool(name="loads", bufs=2))
        values = ctx.enter_context(tc.tile_pool(name="values", bufs=2 * PASSES))
        codes = ctx.enter_context(tc.tile_pool(name="codes", bufs=2))
        stage = ctx.enter_context(tc.tile_pool(name="stage", bufs=3))
        grouped = ctx.enter_context(tc.tile_pool(name="grouped", bufs=PASSES))
        gates = ctx.enter_context(tc.tile_pool(name="gates", bufs=FINISH_LAG + 2))
        logs = ctx.enter_context(tc.tile_pool(name="logs", bufs=TILES_PER_BATCH + 2))
        psum_xt = ctx.enter_context(tc.psum_pool(name="psum_xt", bufs=3))
        psum_et = ctx.enter_context(tc.psum_pool(name="psum_et", bufs=1))
        psum_out = ctx.enter_context(tc.psum_pool(name="psum_out", bufs=4))

        query_loads = {}
        key_loads = {}
        key_exp = {}
        key_codes = {}
        score_codes = {}
        exponents = {}
        transposed = {}
        scores = {}
        node_ps = {}
        node_t = {}
        q_ps = {}
        num_ps = {}
        gate = {}
        log_den = {}

        def is_tile(t):
            return 0 <= t < TILES

        def load_queries(h):
            b, first = divmod(h * LOAD_TILES, TILES_PER_BATCH)
            rows = slice(first, first + LOAD_TILES)
            dist = loads.tile([P, LOAD_TILES, M], BF16, name="dist")
            nc.sync.dma_start(out=dist[:], in_=dist_view[b, :, rows, :])
            mask = loads.tile([P, LOAD_TILES, M], BF16, name="mask")
            nc.sync.dma_start(out=mask[:], in_=mask_view[b, :, rows, :])
            node = loads.tile([P, LOAD_TILES, D], BF16, name="node")
            nc.sync.dma_start(out=node[:], in_=node_view[b, :, rows, :])
            query_loads[h] = (dist, mask, node)

        def load_keys(b, g):
            k_rows = loads.tile([P, PACK, D], BF16, name="k_rows")
            nc.sync.dma_start(out=k_rows[:], in_=k_view[b, g])
            v_rows = values.tile([P, PACK, D], BF16, name="v_rows")
            nc.sync.dma_start(out=v_rows[:], in_=v_view[b, g])
            key_loads[(b, g)] = (k_rows, v_rows)

        def exp_keys(piece):
            b, rest = divmod(piece, PIECES_PER_BATCH)
            g, part = divmod(rest, PIECES_PER_PASS)
            if part == 0:
                ek = stage.tile([P, PACK, D], F32, name="ek")
                key_exp[(b, g)] = ek
            cols = slice(part * PIECE, (part + 1) * PIECE)
            nc.scalar.activation(
                out=key_exp[(b, g)][:, :, cols], in_=key_loads[(b, g)][0][:, :, cols], func=ACT.Exp
            )

        def quantise_keys(b, kind):
            words = codes.tile([P, PASSES, D], U32, name="%s_words" % kind, align_bytes=64)
            scales = codes.tile([P, PASSES, D], U8, name="%s_scales" % kind, align_bytes=64)
            key_codes[(b, kind)] = (words, scales)
            rounded = []
            for g in range(PASSES):
                in_order = grouped.tile([P, D, PACK], BF16, name="%s_in_order" % kind, align_bytes=64)
                out_runs = in_order[:].rearrange("p (a e) j -> p a j e", e=RUN)
                ek_runs = key_exp[(b, g)][:].rearrange("p j (a e) -> p a j e", e=RUN)
                if kind == "ekv":
                    v_runs = key_loads[(b, g)][1][:].rearrange("p j (a e) -> p a j e", e=RUN)
                    nc.vector.tensor_tensor(out=out_runs, in0=ek_runs, in1=v_runs, op=ALU.mult)
                elif b == 0:
                    nc.scalar.copy(out=out_runs, in_=ek_runs)
                else:
                    nc.vector.tensor_copy(out=out_runs, in_=ek_runs)
                rounded.append(in_order)
            for g in range(PASSES):
                nc.vector.quantize_mx(
                    out=words[:, g, :].bitcast(FP8X4),
                    scales=scales[:, g, :],
                    in_=rounded[g][:].rearrange("p d j -> p (d j)"),
                )

        def form_exponents(t):
            dist, mask = query_loads[t // LOAD_TILES][0:2]
            row = t % LOAD_TILES
            exponent = stage.tile([P, M], F32, name="exponent")
            nc.vector.scalar_tensor_tensor(
                out=exponent[:], in0=dist[:, row, :], scalar=neg_slope[:, 0:1],
                in1=mask[:, row, :], op0=ALU.mult, op1=ALU.add,
            )
            exponents[t] = exponent

        def transposes_for(t):
            node = query_loads[t // LOAD_TILES][2]
            row = t % LOAD_TILES
            xts = []
            for g in range(PASSES):
                xt = psum_xt.tile([P, PACK, P], F32, name="xt")
                xts.append(xt)
            et = psum_et.tile([P, F_CHUNKS, P], BF16, name="et")
            transposed[t] = xts
            node_ps[t] = et

            def exponent_block(g, j):
                first = (g * PACK + j) * P
                return lambda: nc.tensor.transpose(
                    xts[g][:, j, :], exponents[t][:, first : first + P], ident_f32[:]
                )

            def node_block(c):
                return lambda: nc.tensor.transpose(
                    et[:, c, :], node[:, row, c * P : (c + 1) * P], ident_bf16[:]
                )

            return (
                [exponent_block(0, j) for j in range(PACK)]
                + [node_block(c) for c in range(F_CHUNKS)]
                + [exponent_block(1, j) for j in range(PACK)]
            )

        def project_and_transpose(t_q, t_next):
            waiting = transposes_for(t_next) if is_tile(t_next) else []
            if is_tile(t_q):
                b, i = divmod(t_q, TILES_PER_BATCH)
                q_acc = psum_out.tile([P, D], F32, name="q_acc", tag="out_bank")
                q_ps[t_q] = q_acc
            for c in range(F_CHUNKS):
                if is_tile(t_q):
                    nc.tensor.matmul(
                        out=q_acc[:], lhsT=node_t[t_q][:, c, :], rhs=wq_t[:, c, :],
                        start=(c == 0), stop=False,
                    )
                for transpose_block in waiting[c * T_PER_MATMUL : (c + 1) * T_PER_MATMUL]:
                    transpose_block()
            if is_tile(t_q):
                nc.tensor.matmul(
                    out=q_acc[:], lhsT=load_by_tile[:, b, i, :], rhs=wq_t[:, F_CHUNKS, :],
                    start=False, stop=True,
                )

        def exp_scores(t):
            eb_grouped = stage.tile([P, PASSES, P, PACK], BF16, name="eb_grouped", align_bytes=64)
            for g in range(PASSES):
                nc.scalar.activation(
                    out=eb_grouped[:, g, :, :],
                    in_=transposed[t][g][:].rearrange("p j r -> p r j"),
                    func=ACT.Exp,
                )
            scores[t] = eb_grouped

        def quantise_scores(t):
            b, i = divmod(t, TILES_PER_BATCH)
            if b not in score_codes:
                eb_codes = codes.tile(
                    [P, TILES_PER_BATCH, PASSES, P], U32, name="eb_codes", align_bytes=64
                )
                eb_scales = codes.tile(
                    [P, TILES_PER_BATCH, PASSES, P], U8, name="eb_scales", align_bytes=64
                )
                score_codes[b] = (eb_codes, eb_scales)
            eb_codes, eb_scales = score_codes[b]
            nc.vector.quantize_mx(
                out=eb_codes[:, i, :, :].rearrange("p g r -> p (g r)").bitcast(FP8X4),
                scales=eb_scales[:, i, :, :].rearrange("p g r -> p (g r)"),
                in_=scores[t][:].rearrange("p g r j -> p (g r j)"),
            )

        def copy_node_t(t, copy):
            node_cols = stage.tile([P, F_CHUNKS, P], BF16, name="node_cols")
            copy(out=node_cols[:], in_=node_ps[t][:])
            node_t[t] = node_cols

        def mix(t, kind):
            b, i = divmod(t, TILES_PER_BATCH)
            eb_codes, eb_scales = score_codes[b]
            key_words, key_scales = key_codes[(b, kind)]
            acc = psum_out.tile([P, D], F32, name="acc", tag="out_bank")
            for g in range(PASSES):
                nc.tensor.matmul_mx(
                    out=acc[:],
                    lhsT=eb_codes[:, i, g, :].bitcast(FP8X4),
                    lhsT_scale=eb_scales[:, i, g, :],
                    rhs=key_words[:, g, :].bitcast(FP8X4),
                    rhs_scale=key_scales[:, g, :],
                    start=(g == 0),
                    stop=(g == PASSES - 1),
                )
            return acc

        def tanh_gate(t):
            gate_t = gates.tile([P, D], F32, name="gate_t")
            nc.scalar.activation(out=gate_t[:], in_=q_ps[t][:], func=ACT.Tanh, scale=0.5)
            gate[t] = gate_t

        def merge_gate_and_num(t):
            nc.vector.scalar_tensor_tensor(
                out=gate[t][:], in0=gate[t][:], scalar=1.0, in1=num_ps[t][:],
                op0=ALU.add, op1=ALU.mult,
            )

        def log_of_den(t):
            den = mix(t, "ek")
            log_t = logs.tile([P, D], F32, name="log_t")
            nc.scalar.activation(out=log_t[:], in_=den[:], func=ACT.Ln)
            log_den[t] = log_t

        def reciprocal_of_den(t):
            nc.scalar.activation(out=log_den[t][:], in_=log_den[t][:], func=ACT.Exp, scale=-1.0)

        def finish(t):
            b, i = divmod(t, TILES_PER_BATCH)
            nc.vector.scalar_tensor_tensor(
                out=gate[t][:], in0=gate[t][:], scalar=0.5, in1=log_den[t][:],
                op0=ALU.mult, op1=ALU.mult,
            )
            nc.sync.dma_start(out=out_view[b, :, i, :], in_=gate[t][:])

        load_rows = consts.tile([P, B * N], BF16, name="load_rows")
        nc.vector.memset(load_rows[:], 0.0)

        alpha_all = consts.tile([P, 1], BF16, name="alpha_all")
        nc.sync.dma_start(out=alpha_all[:], in_=alpha1.partition_broadcast(P))
        scale_all = consts.tile([P, 1], BF16, name="scale_all")
        nc.sync.dma_start(out=scale_all[:], in_=log_scale.partition_broadcast(P))
        for g in range(PASSES):
            load_keys(0, g)
        neg_slope = consts.tile([P, 1], F32, name="neg_slope")
        nc.vector.scalar_tensor_tensor(
            out=neg_slope[:], in0=alpha_all[:], scalar=-1.0, in1=scale_all[:],
            op0=ALU.mult, op1=ALU.mult,
        )

        wq_rows = consts.tile([P, F_CHUNKS, D + 2], BF16, name="wq_rows")
        nc.sync.dma_start(
            out=wq_rows[:, :, 0 : D + 1], in_=Wq_last.rearrange("(r p) f -> p r f", p=P)
        )
        nc.sync.dma_start(
            out=load_rows[P - 1 : P, :], in_=load.rearrange("(o b) n -> o (b n)", o=1)
        )
        load_by_tile = load_rows[:].rearrange("q (b p i) -> q b i p", b=B, i=TILES_PER_BATCH)

        ident_f32 = consts.tile([P, P], F32, name="ident_f32")
        make_identity(nc, ident_f32[:])
        ident_bf16 = consts.tile([P, P], BF16, name="ident_bf16")
        make_identity(nc, ident_bf16[:])

        for piece in range(PIECES_PER_BATCH):
            exp_keys(piece)
        quantise_keys(0, "ekv")
        quantise_keys(0, "ek")

        wq_t = consts.tile([P, F_CHUNKS + 1, D], BF16, name="wq_t")
        for c in range(F_CHUNKS + 1):
            first = min(c * P, D + 1 - P)
            wq_ps = psum_out.tile([P, F_CHUNKS, P], BF16, name="wq_ps", tag="out_bank")
            for r in range(F_CHUNKS):
                nc.tensor.transpose(
                    wq_ps[:, r, :], wq_rows[:, r, first : first + P], ident_bf16[:]
                )
            nc.scalar.copy(out=wq_t[:, c, :], in_=wq_ps[:].rearrange("p r d -> p (r d)"))

        for step in range(FIRST_STEP, LAST_STEP + 1):
            key_load, rest = divmod(step + KEY_LOAD_LEAD, PIECES_PER_PASS)
            if rest == 0 and PASSES <= key_load < B * PASSES:
                load_keys(key_load // PASSES, key_load % PASSES)
            query_load, rest = divmod(step + LOAD_LEAD, LOAD_TILES)
            if rest == 0 and query_load < TILES // LOAD_TILES:
                load_queries(query_load)

            if is_tile(step + EXP_LEAD) and (step + EXP_LEAD) % 2 == 1:
                copy_node_t(step + EXP_LEAD, nc.vector.tensor_copy)
            if is_tile(step - MERGE_LAG):
                merge_gate_and_num(step - MERGE_LAG)
            if is_tile(step):
                quantise_scores(step)
            if is_tile(step + EXPONENT_LEAD):
                form_exponents(step + EXPONENT_LEAD)
            batch, rest = divmod(step, TILES_PER_BATCH)
            if rest == 0 and 1 <= batch < B:
                quantise_keys(batch, "ekv")
                quantise_keys(batch, "ek")
            if is_tile(step - FINISH_LAG):
                finish(step - FINISH_LAG)

            project_and_transpose(step, step + TRANSPOSE_LEAD)
            if is_tile(step - NUM_LAG):
                num_ps[step - NUM_LAG] = mix(step - NUM_LAG, "ekv")

            if is_tile(step + EXP_LEAD) and (step + EXP_LEAD) % 2 == 0:
                copy_node_t(step + EXP_LEAD, nc.scalar.copy)
            if is_tile(step + EXP_LEAD):
                exp_scores(step + EXP_LEAD)
            if is_tile(step - NUM_LAG):
                tanh_gate(step - NUM_LAG)
            if PIECES_PER_BATCH <= step + KEY_LEAD < PIECES:
                exp_keys(step + KEY_LEAD)
            if is_tile(step - RECIP_LAG):
                reciprocal_of_den(step - RECIP_LAG)

            batch, rest = divmod(step + 1, TILES_PER_BATCH)
            if rest == 0 and 1 <= batch <= B:
                for t in range((batch - 1) * TILES_PER_BATCH, batch * TILES_PER_BATCH):
                    log_of_den(t)
